import numpy as np
import ml_dtypes

BF16 = ml_dtypes.bfloat16


def bf(x):
    return np.asarray(x, np.float32).astype(BF16)


def f32(x):
    return np.asarray(x, np.float32)


def f64(x):
    return np.asarray(x).astype(np.float64)


def striped(idx):
    return np.tile(idx.reshape(-1, 16).T, (8, 1))


NX, F, T, P, S, N, H, K = 16, 128, 4, 2, 1024, 4096, 512, 8


def setup_inputs():
    return {
        "x": f32(np.random.standard_normal((P * F, S))),
        "pre": f32(np.random.standard_normal((T * F, NX))),
        "post": f32(np.random.standard_normal((T * F, NX))),
        "ka": f32(np.random.standard_normal((T * F, NX * NX)) / np.sqrt(NX)),
        "kb": f32(np.random.standard_normal((T * F, NX * NX)) / np.sqrt(NX)),
        "offs": striped(np.concatenate([np.random.permutation(S)[:H] for _ in range(K)])),
    }


def reference(x, pre, post, ka, kb, offs):
    idx = offs[:16].T.reshape(-1)
    d = f64(x)[:, idx].reshape(P, 1, F, NX, NX, NX)
    d = np.broadcast_to(d, (P, T // P, F, NX, NX, NX)).reshape(T, F, NX, NX, NX)
    e = d * f64(pre).reshape(T, F, 1, 1, NX)
    h = np.einsum("tfrab,tfbm->tfram", e, f64(kb).reshape(T, F, NX, NX))
    w = f64(post).reshape(T, F, NX, 1) * f64(ka).reshape(T, F, NX, NX)
    return np.einsum("tfram,tfam->frm", h, w).reshape(F, NX * NX)

@@ -1,0 +1,89 @@
+import concourse.mybir as mybir
+
+F32 = mybir.dt.float32
+U16 = mybir.dt.uint16
+MULT = mybir.AluOpType.mult
+ADD = mybir.AluOpType.add
+AXIS_X = mybir.AxisListType.X
+
+F = 128
+T = 4
+NX = 16
+S = 1024
+N = NX * NX * NX
+PIECE = S
+
+FLOPS = T * F * N + 2 * T * F * N * NX + 2 * T * F * NX * NX * NX
+
+
+def tile_multifreqfstar_kernel(tc, x, pre, post, ka, kb, offs, out):
+    nc = tc.nc
+    with (
+        tc.tile_pool(name="held", bufs=1) as held,
+        tc.tile_pool(name="work", bufs=2) as work,
+    ):
+        offsets = held.tile([F, N // 16], U16, name="offsets")
+        nc.sync.dma_start(offsets[:], offs)
+
+        x_part = [held.tile([F, S], F32, name=f"x_part{p}") for p in range(2)]
+        for p in range(2):
+            nc.sync.dma_start(x_part[p][:], x[p * F : (p + 1) * F, :])
+
+        pre_sb = held.tile([F, T, NX], F32, name="pre_sb")
+        post_sb = held.tile([F, T, NX], F32, name="post_sb")
+        ka_sb = held.tile([F, T, NX, NX], F32, name="ka_sb")
+        kb_sb = held.tile([F, T, NX, NX], F32, name="kb_sb")
+        nc.scalar.dma_start(pre_sb[:], pre.rearrange("(t f) b -> f t b", f=F))
+        nc.scalar.dma_start(post_sb[:], post.rearrange("(t f) a -> f t a", f=F))
+        nc.scalar.dma_start(ka_sb[:], ka.rearrange("(t f) (a m) -> f t a m", f=F, m=NX))
+        nc.scalar.dma_start(kb_sb[:], kb.rearrange("(t f) (b m) -> f t b m", f=F, m=NX))
+
+        post_ka = held.tile([F, T, NX, NX], F32, name="post_ka")
+        nc.gpsimd.tensor_tensor(
+            post_ka[:],
+            ka_sb[:].rearrange("f t a m -> f t m a"),
+            post_sb[:].unsqueeze(2).to_broadcast([F, T, NX, NX]),
+            MULT,
+        )
+        kb_mb = held.tile([F, T, NX, NX], F32, name="kb_mb")
+        nc.gpsimd.tensor_copy(kb_mb[:], kb_sb[:].rearrange("f t b m -> f t m b"))
+
+        pre_wide = held.tile([F, T, PIECE // NX, NX], F32, name="pre_wide")
+        nc.gpsimd.tensor_copy(pre_wide[:], pre_sb[:].unsqueeze(2).to_broadcast([F, T, PIECE // NX, NX]))
+
+        partial = held.tile([F, T, NX, NX], F32, name="partial")
+        for t in range(T):
+            pair = work.tile([F, NX, NX, NX], F32, name="pair")
+            nc.gpsimd.tensor_tensor(
+                pair[:],
+                kb_mb[:, t].unsqueeze(2).to_broadcast([F, NX, NX, NX]),
+                post_ka[:, t].unsqueeze(3).to_broadcast([F, NX, NX, NX]),
+                MULT,
+            )
+
+            e = work.tile([F, N // NX, NX], F32, name="e")
+            for q in range(N // PIECE):
+                rows = PIECE // NX
+                nc.vector.tensor_tensor(
+                    e[:, q * rows : (q + 1) * rows, :],
+                    x_part[t // 2][:].indirect(offsets[:, q * (PIECE // 16) : (q + 1) * (PIECE // 16)]),
+                    pre_wide[:, t],
+                    MULT,
+                )
+
+            for r in range(NX):
+                product = work.tile([F, NX, NX * NX], F32, name="product")
+                nc.vector.tensor_tensor(
+                    product[:],
+                    e[:, r * NX : (r + 1) * NX, :]
+                    .rearrange("f a b -> f (a b)")
+                    .unsqueeze(1)
+                    .to_broadcast([F, NX, NX * NX]),
+                    pair[:].rearrange("f m a b -> f m (a b)"),
+                    MULT,
+                )
+                nc.vector.tensor_reduce(partial[:, t, r, :], product[:], AXIS_X, ADD)
+
+        total = held.tile([F, NX * NX], F32, name="total")
+        nc.vector.tensor_reduce(total[:], partial[:].rearrange("f t r m -> f (r m) t"), AXIS_X, ADD)
+        nc.sync.dma_start(out, total[:])

@@ -1,10 +1,12 @@
 import concourse.mybir as mybir
+from concourse.masks import make_identity
 
 F32 = mybir.dt.float32
 U16 = mybir.dt.uint16
 MULT = mybir.AluOpType.mult
 ADD = mybir.AluOpType.add
 AXIS_X = mybir.AxisListType.X
+COPY = mybir.ActivationFunctionType.Copy
 
 F = 128
 T = 4
@@ -12,15 +14,35 @@ NX = 16
 S = 1024
 N = NX * NX * NX
 PIECE = S
+K = 128
+HALVES = NX * NX // K
+A_HALF = NX // HALVES
+TILE = 32
+COL_TILES = F // TILE
+FG = TILE // NX
+G = F // FG
+SLOTS = G // COL_TILES
+BANK = 512
+FLIPS = BANK // F
 
 FLOPS = T * F * N + 2 * T * F * N * NX + 2 * T * F * NX * NX * NX
+
+
+def flip_and_group(nc, flips, identity, blocks, grouped):
+    bank = flips.tile([K, FLIPS, F], F32, name="bank")
+    for i, block in enumerate(blocks):
+        nc.tensor.transpose(bank[:, i, :], block, identity[:])
+    nc.scalar.activation(grouped, bank[:].rearrange("k i (g e) -> k g i e", e=FG), COPY)
 
 
 def tile_multifreqfstar_kernel(tc, x, pre, post, ka, kb, offs, out):
     nc = tc.nc
     with (
         tc.tile_pool(name="held", bufs=1) as held,
-        tc.tile_pool(name="work", bufs=2) as work,
+        tc.tile_pool(name="work", bufs=4) as work,
+        tc.tile_pool(name="flipped", bufs=2) as flipped,
+        tc.psum_pool(name="sums", bufs=1) as sums,
+        tc.psum_pool(name="flips", bufs=6) as flips,
     ):
         offsets = held.tile([F, N // 16], U16, name="offsets")
         nc.sync.dma_start(offsets[:], offs)
@@ -34,10 +56,16 @@ def tile_multifreqfstar_kernel(tc, x, pre, post, ka, kb, offs, out):
         ka_sb = held.tile([F, T, NX, NX], F32, name="ka_sb")
         kb_sb = held.tile([F, T, NX, NX], F32, name="kb_sb")
         nc.scalar.dma_start(pre_sb[:], pre.rearrange("(t f) b -> f t b", f=F))
+        nc.scalar.dma_start(kb_sb[:], kb.rearrange("(t f) (b m) -> f t b m", f=F, m=NX))
         nc.scalar.dma_start(post_sb[:], post.rearrange("(t f) a -> f t a", f=F))
         nc.scalar.dma_start(ka_sb[:], ka.rearrange("(t f) (a m) -> f t a m", f=F, m=NX))
-        nc.scalar.dma_start(kb_sb[:], kb.rearrange("(t f) (b m) -> f t b m", f=F, m=NX))
 
+        pre_wide = held.tile([F, T, PIECE // NX, NX], F32, name="pre_wide")
+        for t in range(T):
+            nc.scalar.activation(pre_wide[:, t], pre_sb[:, t].unsqueeze(1).to_broadcast([F, PIECE // NX, NX]), COPY)
+
+        kb_mb = held.tile([F, T, NX, NX], F32, name="kb_mb")
+        nc.scalar.activation(kb_mb[:], kb_sb[:].rearrange("f t b m -> f t m b"), COPY)
         post_ka = held.tile([F, T, NX, NX], F32, name="post_ka")
         nc.gpsimd.tensor_tensor(
             post_ka[:],
@@ -45,45 +73,79 @@ def tile_multifreqfstar_kernel(tc, x, pre, post, ka, kb, offs, out):
             post_sb[:].unsqueeze(2).to_broadcast([F, T, NX, NX]),
             MULT,
         )
-        kb_mb = held.tile([F, T, NX, NX], F32, name="kb_mb")
-        nc.gpsimd.tensor_copy(kb_mb[:], kb_sb[:].rearrange("f t b m -> f t m b"))
 
-        pre_wide = held.tile([F, T, PIECE // NX, NX], F32, name="pre_wide")
-        nc.gpsimd.tensor_copy(pre_wide[:], pre_sb[:].unsqueeze(2).to_broadcast([F, T, PIECE // NX, NX]))
+        identity = held.tile([F, F], F32, name="identity")
+        make_identity(nc, identity[:])
+        own = held.tile([F, FG], F32, name="own")
+        nc.vector.tensor_reduce(own[:], identity[:].rearrange("p (r e) -> p e r", e=FG), AXIS_X, ADD)
 
-        partial = held.tile([F, T, NX, NX], F32, name="partial")
+        zeros = held.tile([K, BANK], F32, name="zeros")
+        nc.gpsimd.memset(zeros[:], 0.0)
+        products = sums.tile([F, SLOTS, NX * FG], F32, name="products")
+        nc.tensor.matmul(products[:].rearrange("p s c -> p (s c)"), zeros[:, 0:F], zeros[:], start=True, stop=False)
+
         for t in range(T):
-            pair = work.tile([F, NX, NX, NX], F32, name="pair")
-            nc.gpsimd.tensor_tensor(
-                pair[:],
-                kb_mb[:, t].unsqueeze(2).to_broadcast([F, NX, NX, NX]),
-                post_ka[:, t].unsqueeze(3).to_broadcast([F, NX, NX, NX]),
-                MULT,
-            )
-
-            e = work.tile([F, N // NX, NX], F32, name="e")
+            e_flipped = flipped.tile([K, HALVES, G, NX, FG], F32, name="e_flipped")
             for q in range(N // PIECE):
-                rows = PIECE // NX
+                e = work.tile([F, FLIPS, HALVES, K], F32, name="e")
                 nc.vector.tensor_tensor(
-                    e[:, q * rows : (q + 1) * rows, :],
+                    e[:].rearrange("f r h k -> f (r h k)"),
                     x_part[t // 2][:].indirect(offsets[:, q * (PIECE // 16) : (q + 1) * (PIECE // 16)]),
-                    pre_wide[:, t],
+                    pre_wide[:, t].rearrange("f c b -> f (c b)"),
                     MULT,
                 )
+                for half in range(HALVES):
+                    flip_and_group(
+                        nc,
+                        flips,
+                        identity,
+                        [e[:, i, half, :] for i in range(FLIPS)],
+                        e_flipped[:, half, :, q * FLIPS : (q + 1) * FLIPS, :],
+                    )
 
-            for r in range(NX):
-                product = work.tile([F, NX, NX * NX], F32, name="product")
-                nc.vector.tensor_tensor(
-                    product[:],
-                    e[:, r * NX : (r + 1) * NX, :]
-                    .rearrange("f a b -> f (a b)")
-                    .unsqueeze(1)
-                    .to_broadcast([F, NX, NX * NX]),
-                    pair[:].rearrange("f m a b -> f m (a b)"),
+            pair_flipped = flipped.tile([K, HALVES, G, NX, FG], F32, name="pair_flipped")
+            for half in range(HALVES):
+                pair = work.tile([F, NX, A_HALF, NX], F32, name="pair")
+                nc.gpsimd.tensor_tensor(
+                    pair[:],
+                    kb_mb[:, t].unsqueeze(2).to_broadcast([F, NX, A_HALF, NX]),
+                    post_ka[:, t, :, half * A_HALF : (half + 1) * A_HALF].unsqueeze(3).to_broadcast([F, NX, A_HALF, NX]),
                     MULT,
                 )
-                nc.vector.tensor_reduce(partial[:, t, r, :], product[:], AXIS_X, ADD)
+                for m in range(0, NX, FLIPS):
+                    flip_and_group(
+                        nc,
+                        flips,
+                        identity,
+                        [pair[:, m + i].rearrange("f a b -> f (a b)") for i in range(FLIPS)],
+                        pair_flipped[:, half, :, m : m + FLIPS, :],
+                    )
 
-        total = held.tile([F, NX * NX], F32, name="total")
-        nc.vector.tensor_reduce(total[:], partial[:].rearrange("f t r m -> f (r m) t"), AXIS_X, ADD)
-        nc.sync.dma_start(out, total[:])
+            for half in range(HALVES):
+                for slot in range(SLOTS):
+                    for j in range(COL_TILES):
+                        g = slot * COL_TILES + j
+                        nc.tensor.matmul(
+                            products[j * TILE : (j + 1) * TILE, slot, :],
+                            e_flipped[:, half, g].rearrange("k r e -> k (r e)"),
+                            pair_flipped[:, half, g].rearrange("k m e -> k (m e)"),
+                            start=False,
+                            stop=(t == T - 1 and half == HALVES - 1 and slot == SLOTS - 1),
+                        )
+
+        kept = held.tile([F, SLOTS * NX, FG], F32, name="kept")
+        nc.vector.tensor_tensor(
+            kept[:],
+            products[:].rearrange("p s (m e) -> p (s m) e", e=FG),
+            own[:].unsqueeze(1).to_broadcast([F, SLOTS * NX, FG]),
+            MULT,
+        )
+        result = held.tile([F, SLOTS, NX], F32, name="result")
+        nc.vector.tensor_reduce(result[:].rearrange("p s m -> p (s m)"), kept[:], AXIS_X, ADD)
+
+        out_rows = out.rearrange("(s j e) (r m) -> j e r s m", j=COL_TILES, e=FG, m=NX)
+        result_rows = result[:].rearrange("(j r e) s m -> j e r s m", j=COL_TILES, e=FG)
+        for j in range(COL_TILES):
+            for f in range(FG):
+                queue = nc.sync if f % 2 == 0 else nc.scalar
+                queue.dma_start(out_rows[j, f], result_rows[j, f])

@@ -67,7 +67,7 @@ def tile_multifreqfstar_kernel(tc, x, pre, post, ka, kb, offs, out):
         kb_mb = held.tile([F, T, NX, NX], F32, name="kb_mb")
         nc.scalar.activation(kb_mb[:], kb_sb[:].rearrange("f t b m -> f t m b"), COPY)
         post_ka = held.tile([F, T, NX, NX], F32, name="post_ka")
-        nc.gpsimd.tensor_tensor(
+        nc.vector.tensor_tensor(
             post_ka[:],
             ka_sb[:].rearrange("f t a m -> f t m a"),
             post_sb[:].unsqueeze(2).to_broadcast([F, T, NX, NX]),
@@ -85,6 +85,24 @@ def tile_multifreqfstar_kernel(tc, x, pre, post, ka, kb, offs, out):
         nc.tensor.matmul(products[:].rearrange("p s c -> p (s c)"), zeros[:, 0:F], zeros[:], start=True, stop=False)
 
         for t in range(T):
+            pair_flipped = flipped.tile([K, HALVES, G, NX, FG], F32, name="pair_flipped")
+            for half in range(HALVES):
+                pair = work.tile([F, NX, A_HALF, NX], F32, name="pair")
+                nc.vector.tensor_tensor(
+                    pair[:],
+                    kb_mb[:, t].unsqueeze(2).to_broadcast([F, NX, A_HALF, NX]),
+                    post_ka[:, t, :, half * A_HALF : (half + 1) * A_HALF].unsqueeze(3).to_broadcast([F, NX, A_HALF, NX]),
+                    MULT,
+                )
+                for m in range(0, NX, FLIPS):
+                    flip_and_group(
+                        nc,
+                        flips,
+                        identity,
+                        [pair[:, m + i].rearrange("f a b -> f (a b)") for i in range(FLIPS)],
+                        pair_flipped[:, half, :, m : m + FLIPS, :],
+                    )
+
             e_flipped = flipped.tile([K, HALVES, G, NX, FG], F32, name="e_flipped")
             for q in range(N // PIECE):
                 e = work.tile([F, FLIPS, HALVES, K], F32, name="e")
@@ -101,24 +119,6 @@ def tile_multifreqfstar_kernel(tc, x, pre, post, ka, kb, offs, out):
                         identity,
                         [e[:, i, half, :] for i in range(FLIPS)],
                         e_flipped[:, half, :, q * FLIPS : (q + 1) * FLIPS, :],
-                    )
-
-            pair_flipped = flipped.tile([K, HALVES, G, NX, FG], F32, name="pair_flipped")
-            for half in range(HALVES):
-                pair = work.tile([F, NX, A_HALF, NX], F32, name="pair")
-                nc.gpsimd.tensor_tensor(
-                    pair[:],
-                    kb_mb[:, t].unsqueeze(2).to_broadcast([F, NX, A_HALF, NX]),
-                    post_ka[:, t, :, half * A_HALF : (half + 1) * A_HALF].unsqueeze(3).to_broadcast([F, NX, A_HALF, NX]),
-                    MULT,
-                )
-                for m in range(0, NX, FLIPS):
-                    flip_and_group(
-                        nc,
-                        flips,
-                        identity,
-                        [pair[:, m + i].rearrange("f a b -> f (a b)") for i in range(FLIPS)],
-                        pair_flipped[:, half, :, m : m + FLIPS, :],
                     )
 
             for half in range(HALVES):

@@ -4,12 +4,11 @@ from concourse.masks import make_identity
 F32 = mybir.dt.float32
 U16 = mybir.dt.uint16
 MULT = mybir.AluOpType.mult
-ADD = mybir.AluOpType.add
-AXIS_X = mybir.AxisListType.X
 COPY = mybir.ActivationFunctionType.Copy
 
 F = 128
 T = 4
+TERMS_OF_PART = 2
 NX = 16
 S = 1024
 N = NX * NX * NX
@@ -39,7 +38,8 @@ def tile_multifreqfstar_kernel(tc, x, pre, post, ka, kb, offs, out):
     nc = tc.nc
     with (
         tc.tile_pool(name="held", bufs=1) as held,
-        tc.tile_pool(name="work", bufs=4) as work,
+        tc.tile_pool(name="terms", bufs=2) as terms,
+        tc.tile_pool(name="work", bufs=6) as work,
         tc.tile_pool(name="flipped", bufs=2) as flipped,
         tc.psum_pool(name="sums", bufs=1) as sums,
         tc.psum_pool(name="flips", bufs=6) as flips,
@@ -47,37 +47,13 @@ def tile_multifreqfstar_kernel(tc, x, pre, post, ka, kb, offs, out):
         offsets = held.tile([F, N // 16], U16, name="offsets")
         nc.sync.dma_start(offsets[:], offs)
 
-        x_part = [held.tile([F, S], F32, name=f"x_part{p}") for p in range(2)]
-        for p in range(2):
-            nc.sync.dma_start(x_part[p][:], x[p * F : (p + 1) * F, :])
-
         pre_sb = held.tile([F, T, NX], F32, name="pre_sb")
         post_sb = held.tile([F, T, NX], F32, name="post_sb")
-        ka_sb = held.tile([F, T, NX, NX], F32, name="ka_sb")
-        kb_sb = held.tile([F, T, NX, NX], F32, name="kb_sb")
         nc.scalar.dma_start(pre_sb[:], pre.rearrange("(t f) b -> f t b", f=F))
-        nc.scalar.dma_start(kb_sb[:], kb.rearrange("(t f) (b m) -> f t b m", f=F, m=NX))
         nc.scalar.dma_start(post_sb[:], post.rearrange("(t f) a -> f t a", f=F))
-        nc.scalar.dma_start(ka_sb[:], ka.rearrange("(t f) (a m) -> f t a m", f=F, m=NX))
-
-        pre_wide = held.tile([F, T, PIECE // NX, NX], F32, name="pre_wide")
-        for t in range(T):
-            nc.scalar.activation(pre_wide[:, t], pre_sb[:, t].unsqueeze(1).to_broadcast([F, PIECE // NX, NX]), COPY)
-
-        kb_mb = held.tile([F, T, NX, NX], F32, name="kb_mb")
-        nc.scalar.activation(kb_mb[:], kb_sb[:].rearrange("f t b m -> f t m b"), COPY)
-        post_ka = held.tile([F, T, NX, NX], F32, name="post_ka")
-        nc.vector.tensor_tensor(
-            post_ka[:],
-            ka_sb[:].rearrange("f t a m -> f t m a"),
-            post_sb[:].unsqueeze(2).to_broadcast([F, T, NX, NX]),
-            MULT,
-        )
 
         identity = held.tile([F, F], F32, name="identity")
         make_identity(nc, identity[:])
-        own = held.tile([F, FG], F32, name="own")
-        nc.vector.tensor_reduce(own[:], identity[:].rearrange("p (r e) -> p e r", e=FG), AXIS_X, ADD)
 
         zeros = held.tile([K, BANK], F32, name="zeros")
         nc.gpsimd.memset(zeros[:], 0.0)
@@ -85,13 +61,33 @@ def tile_multifreqfstar_kernel(tc, x, pre, post, ka, kb, offs, out):
         nc.tensor.matmul(products[:].rearrange("p s c -> p (s c)"), zeros[:, 0:F], zeros[:], start=True, stop=False)
 
         for t in range(T):
+            kb_sb = terms.tile([F, NX, NX], F32, name="kb_sb")
+            ka_sb = terms.tile([F, NX, NX], F32, name="ka_sb")
+            nc.sync.dma_start(kb_sb[:], kb[t * F : (t + 1) * F, :].rearrange("f (b m) -> f b m", m=NX))
+            nc.sync.dma_start(ka_sb[:], ka[t * F : (t + 1) * F, :].rearrange("f (a m) -> f a m", m=NX))
+            if t % TERMS_OF_PART == 0:
+                x_part = held.tile([F, S], F32, name=f"x_part{t // TERMS_OF_PART}")
+                nc.sync.dma_start(x_part[:], x[(t // TERMS_OF_PART) * F : (t // TERMS_OF_PART + 1) * F, :])
+
+            kb_mb = terms.tile([F, NX, NX], F32, name="kb_mb")
+            nc.scalar.activation(kb_mb[:], kb_sb[:].rearrange("f b m -> f m b"), COPY)
+            pre_wide = terms.tile([F, PIECE // NX, NX], F32, name="pre_wide")
+            nc.scalar.activation(pre_wide[:], pre_sb[:, t].unsqueeze(1).to_broadcast([F, PIECE // NX, NX]), COPY)
+
+            post_ka = terms.tile([F, NX, NX], F32, name="post_ka")
+            nc.vector.tensor_tensor(
+                post_ka[:],
+                ka_sb[:].rearrange("f a m -> f m a"),
+                post_sb[:, t].unsqueeze(1).to_broadcast([F, NX, NX]),
+                MULT,
+            )
             pair_flipped = flipped.tile([K, HALVES, G, NX, FG], F32, name="pair_flipped")
             for half in range(HALVES):
                 pair = work.tile([F, NX, A_HALF, NX], F32, name="pair")
                 nc.vector.tensor_tensor(
                     pair[:],
-                    kb_mb[:, t].unsqueeze(2).to_broadcast([F, NX, A_HALF, NX]),
-                    post_ka[:, t, :, half * A_HALF : (half + 1) * A_HALF].unsqueeze(3).to_broadcast([F, NX, A_HALF, NX]),
+                    kb_mb[:].unsqueeze(2).to_broadcast([F, NX, A_HALF, NX]),
+                    post_ka[:, :, half * A_HALF : (half + 1) * A_HALF].unsqueeze(3).to_broadcast([F, NX, A_HALF, NX]),
                     MULT,
                 )
                 for m in range(0, NX, FLIPS):
@@ -108,8 +104,8 @@ def tile_multifreqfstar_kernel(tc, x, pre, post, ka, kb, offs, out):
                 e = work.tile([F, FLIPS, HALVES, K], F32, name="e")
                 nc.vector.tensor_tensor(
                     e[:].rearrange("f r h k -> f (r h k)"),
-                    x_part[t // 2][:].indirect(offsets[:, q * (PIECE // 16) : (q + 1) * (PIECE // 16)]),
-                    pre_wide[:, t].rearrange("f c b -> f (c b)"),
+                    x_part[:].indirect(offsets[:, q * (PIECE // 16) : (q + 1) * (PIECE // 16)]),
+                    pre_wide[:].rearrange("f c b -> f (c b)"),
                     MULT,
                 )
                 for half in range(HALVES):
@@ -128,24 +124,19 @@ def tile_multifreqfstar_kernel(tc, x, pre, post, ka, kb, offs, out):
                         nc.tensor.matmul(
                             products[j * TILE : (j + 1) * TILE, slot, :],
                             e_flipped[:, half, g].rearrange("k r e -> k (r e)"),
-                            pair_flipped[:, half, g].rearrange("k m e -> k (m e)"),
+                            pair_flipped[:, half, g].rearrange("k m e -> k e m"),
                             start=False,
                             stop=(t == T - 1 and half == HALVES - 1 and slot == SLOTS - 1),
                         )
 
-        kept = held.tile([F, SLOTS * NX, FG], F32, name="kept")
-        nc.vector.tensor_tensor(
-            kept[:],
-            products[:].rearrange("p s (m e) -> p (s m) e", e=FG),
-            own[:].unsqueeze(1).to_broadcast([F, SLOTS * NX, FG]),
-            MULT,
+        result = held.tile([F, SLOTS, FG, NX], F32, name="result")
+        nc.scalar.activation(
+            result[:].rearrange("p s e m -> p (s e m)"), products[:].rearrange("p s c -> p (s c)"), COPY
         )
-        result = held.tile([F, SLOTS, NX], F32, name="result")
-        nc.vector.tensor_reduce(result[:].rearrange("p s m -> p (s m)"), kept[:], AXIS_X, ADD)
 
         out_rows = out.rearrange("(s j e) (r m) -> j e r s m", j=COL_TILES, e=FG, m=NX)
-        result_rows = result[:].rearrange("(j r e) s m -> j e r s m", j=COL_TILES, e=FG)
+        result_rows = result[:].rearrange("(j r e) s c m -> j e r s c m", j=COL_TILES, e=FG)
         for j in range(COL_TILES):
             for f in range(FG):
                 queue = nc.sync if f % 2 == 0 else nc.scalar
-                queue.dma_start(out_rows[j, f], result_rows[j, f])
+                queue.dma_start(out_rows[j, f], result_rows[j, f, :, :, f, :])

@@ -42,6 +42,7 @@ def tile_multifreqfstar_kernel(tc, x, pre, post, ka, kb, offs, out):
         tc.tile_pool(name="work", bufs=6) as work,
         tc.tile_pool(name="flipped", bufs=2) as flipped,
         tc.psum_pool(name="sums", bufs=1) as sums,
+        tc.psum_pool(name="staged", bufs=1) as staged,
         tc.psum_pool(name="flips", bufs=6) as flips,
     ):
         offsets = held.tile([F, N // 16], U16, name="offsets")
@@ -71,6 +72,8 @@ def tile_multifreqfstar_kernel(tc, x, pre, post, ka, kb, offs, out):
 
             kb_mb = terms.tile([F, NX, NX], F32, name="kb_mb")
             nc.scalar.activation(kb_mb[:], kb_sb[:].rearrange("f b m -> f m b"), COPY)
+            kb_bank = staged.tile([F, NX, NX], F32, name="kb_bank")
+            nc.tensor.matmul(kb_bank[:], identity[:], kb_sb[:].rearrange("f b m -> f m b"), start=True, stop=True)
             pre_wide = terms.tile([F, PIECE // NX, NX], F32, name="pre_wide")
             nc.scalar.activation(pre_wide[:], pre_sb[:, t].unsqueeze(1).to_broadcast([F, PIECE // NX, NX]), COPY)
 
@@ -83,19 +86,28 @@ def tile_multifreqfstar_kernel(tc, x, pre, post, ka, kb, offs, out):
             )
             pair_flipped = flipped.tile([K, HALVES, G, NX, FG], F32, name="pair_flipped")
             for half in range(HALVES):
-                pair = work.tile([F, NX, A_HALF, NX], F32, name="pair")
+                a_range = slice(half * A_HALF, (half + 1) * A_HALF)
+                pair_one = work.tile([F, FLIPS, A_HALF, NX], F32, name="pair_one")
+                nc.gpsimd.tensor_tensor(
+                    pair_one[:],
+                    kb_mb[:, 0:FLIPS].unsqueeze(2).to_broadcast([F, FLIPS, A_HALF, NX]),
+                    post_ka[:, 0:FLIPS, a_range].unsqueeze(3).to_broadcast([F, FLIPS, A_HALF, NX]),
+                    MULT,
+                )
+                pair_three = work.tile([F, NX - FLIPS, A_HALF, NX], F32, name="pair_three")
                 nc.vector.tensor_tensor(
-                    pair[:],
-                    kb_mb[:].unsqueeze(2).to_broadcast([F, NX, A_HALF, NX]),
-                    post_ka[:, :, half * A_HALF : (half + 1) * A_HALF].unsqueeze(3).to_broadcast([F, NX, A_HALF, NX]),
+                    pair_three[:],
+                    kb_bank[:, FLIPS:NX].unsqueeze(2).to_broadcast([F, NX - FLIPS, A_HALF, NX]),
+                    post_ka[:, FLIPS:NX, a_range].unsqueeze(3).to_broadcast([F, NX - FLIPS, A_HALF, NX]),
                     MULT,
                 )
                 for m in range(0, NX, FLIPS):
+                    rows = pair_one if m == 0 else pair_three[:, m - FLIPS : m]
                     flip_and_group(
                         nc,
                         flips,
                         identity,
-                        [pair[:, m + i].rearrange("f a b -> f (a b)") for i in range(FLIPS)],
+                        [rows[:, i].rearrange("f a b -> f (a b)") for i in range(FLIPS)],
                         pair_flipped[:, half, :, m : m + FLIPS, :],
                     )
 

@@ -42,8 +42,8 @@ def tile_multifreqfstar_kernel(tc, x, pre, post, ka, kb, offs, out):
         tc.tile_pool(name="work", bufs=6) as work,
         tc.tile_pool(name="flipped", bufs=2) as flipped,
         tc.psum_pool(name="sums", bufs=1) as sums,
-        tc.psum_pool(name="staged", bufs=1) as staged,
-        tc.psum_pool(name="flips", bufs=6) as flips,
+        tc.psum_pool(name="staged", bufs=2) as staged,
+        tc.psum_pool(name="flips", bufs=5) as flips,
     ):
         offsets = held.tile([F, N // 16], U16, name="offsets")
         nc.sync.dma_start(offsets[:], offs)
@@ -61,21 +61,25 @@ def tile_multifreqfstar_kernel(tc, x, pre, post, ka, kb, offs, out):
         products = sums.tile([F, SLOTS, NX * FG], F32, name="products")
         nc.tensor.matmul(products[:].rearrange("p s c -> p (s c)"), zeros[:, 0:F], zeros[:], start=True, stop=False)
 
-        for t in range(T):
+        def stage(t):
             kb_sb = terms.tile([F, NX, NX], F32, name="kb_sb")
             ka_sb = terms.tile([F, NX, NX], F32, name="ka_sb")
             nc.sync.dma_start(kb_sb[:], kb[t * F : (t + 1) * F, :].rearrange("f (b m) -> f b m", m=NX))
             nc.sync.dma_start(ka_sb[:], ka[t * F : (t + 1) * F, :].rearrange("f (a m) -> f a m", m=NX))
             if t % TERMS_OF_PART == 0:
-                x_part = held.tile([F, S], F32, name=f"x_part{t // TERMS_OF_PART}")
-                nc.sync.dma_start(x_part[:], x[(t // TERMS_OF_PART) * F : (t // TERMS_OF_PART + 1) * F, :])
-
+                nc.sync.dma_start(x_part[t // TERMS_OF_PART][:], x[(t // TERMS_OF_PART) * F : (t // TERMS_OF_PART + 1) * F, :])
             kb_mb = terms.tile([F, NX, NX], F32, name="kb_mb")
             nc.scalar.activation(kb_mb[:], kb_sb[:].rearrange("f b m -> f m b"), COPY)
             kb_bank = staged.tile([F, NX, NX], F32, name="kb_bank")
             nc.tensor.matmul(kb_bank[:], identity[:], kb_sb[:].rearrange("f b m -> f m b"), start=True, stop=True)
             pre_wide = terms.tile([F, PIECE // NX, NX], F32, name="pre_wide")
             nc.scalar.activation(pre_wide[:], pre_sb[:, t].unsqueeze(1).to_broadcast([F, PIECE // NX, NX]), COPY)
+            return ka_sb, kb_mb, kb_bank, pre_wide
+
+        x_part = [held.tile([F, S], F32, name=f"x_part{p}") for p in range(T // TERMS_OF_PART)]
+        staged_next = stage(0)
+        for t in range(T):
+            ka_sb, kb_mb, kb_bank, pre_wide = staged_next
 
             post_ka = terms.tile([F, NX, NX], F32, name="post_ka")
             nc.vector.tensor_tensor(
@@ -111,12 +115,15 @@ def tile_multifreqfstar_kernel(tc, x, pre, post, ka, kb, offs, out):
                         pair_flipped[:, half, :, m : m + FLIPS, :],
                     )
 
+            if t + 1 < T:
+                staged_next = stage(t + 1)
+
             e_flipped = flipped.tile([K, HALVES, G, NX, FG], F32, name="e_flipped")
             for q in range(N // PIECE):
                 e = work.tile([F, FLIPS, HALVES, K], F32, name="e")
                 nc.vector.tensor_tensor(
                     e[:].rearrange("f r h k -> f (r h k)"),
-                    x_part[:].indirect(offsets[:, q * (PIECE // 16) : (q + 1) * (PIECE // 16)]),
+                    x_part[t // TERMS_OF_PART][:].indirect(offsets[:, q * (PIECE // 16) : (q + 1) * (PIECE // 16)]),
                     pre_wide[:].rearrange("f c b -> f (c b)"),
                     MULT,
                 )

@@ -23,6 +23,7 @@ G = F // FG
 SLOTS = G // COL_TILES
 BANK = 512
 FLIPS = BANK // F
+STEPS = N // PIECE
 
 FLOPS = T * F * N + 2 * T * F * N * NX + 2 * T * F * NX * NX * NX
 
@@ -76,8 +77,22 @@ def tile_multifreqfstar_kernel(tc, x, pre, post, ka, kb, offs, out):
             nc.scalar.activation(pre_wide[:], pre_sb[:, t].unsqueeze(1).to_broadcast([F, PIECE // NX, NX]), COPY)
             return ka_sb, kb_mb, kb_bank, pre_wide
 
+        def multiply(t, step, e_flipped, pair_flipped):
+            for half in range(HALVES):
+                for slot in range(step * SLOTS // STEPS, (step + 1) * SLOTS // STEPS):
+                    for j in range(COL_TILES):
+                        g = slot * COL_TILES + j
+                        nc.tensor.matmul(
+                            products[j * TILE : (j + 1) * TILE, slot, :],
+                            e_flipped[:, half, g].rearrange("k r e -> k (r e)"),
+                            pair_flipped[:, half, g].rearrange("k m e -> k e m"),
+                            start=False,
+                            stop=(t == T - 1 and half == HALVES - 1 and slot == SLOTS - 1),
+                        )
+
         x_part = [held.tile([F, S], F32, name=f"x_part{p}") for p in range(T // TERMS_OF_PART)]
         staged_next = stage(0)
+        flipped_before = None
         for t in range(T):
             ka_sb, kb_mb, kb_bank, pre_wide = staged_next
 
@@ -135,18 +150,12 @@ def tile_multifreqfstar_kernel(tc, x, pre, post, ka, kb, offs, out):
                         [e[:, i, half, :] for i in range(FLIPS)],
                         e_flipped[:, half, :, q * FLIPS : (q + 1) * FLIPS, :],
                     )
+                if t > 0:
+                    multiply(t - 1, q, *flipped_before)
+            flipped_before = (e_flipped, pair_flipped)
 
-            for half in range(HALVES):
-                for slot in range(SLOTS):
-                    for j in range(COL_TILES):
-                        g = slot * COL_TILES + j
-                        nc.tensor.matmul(
-                            products[j * TILE : (j + 1) * TILE, slot, :],
-                            e_flipped[:, half, g].rearrange("k r e -> k (r e)"),
-                            pair_flipped[:, half, g].rearrange("k m e -> k e m"),
-                            start=False,
-                            stop=(t == T - 1 and half == HALVES - 1 and slot == SLOTS - 1),
-                        )
+        for step in range(STEPS):
+            multiply(T - 1, step, *flipped_before)
 
         result = held.tile([F, SLOTS, FG, NX], F32, name="result")
         nc.scalar.activation(

@@ -24,6 +24,8 @@ SLOTS = G // COL_TILES
 BANK = 512
 FLIPS = BANK // F
 STEPS = N // PIECE
+M_GPSIMD = 5
+M_VECTOR = NX - M_GPSIMD
 
 FLOPS = T * F * N + 2 * T * F * N * NX + 2 * T * F * NX * NX * NX
 
@@ -69,10 +71,11 @@ def tile_multifreqfstar_kernel(tc, x, pre, post, ka, kb, offs, out):
             nc.sync.dma_start(ka_sb[:], ka[t * F : (t + 1) * F, :].rearrange("f (a m) -> f a m", m=NX))
             if t % TERMS_OF_PART == 0:
                 nc.sync.dma_start(x_part[t // TERMS_OF_PART][:], x[(t // TERMS_OF_PART) * F : (t // TERMS_OF_PART + 1) * F, :])
-            kb_mb = terms.tile([F, NX, NX], F32, name="kb_mb")
-            nc.scalar.activation(kb_mb[:], kb_sb[:].rearrange("f b m -> f m b"), COPY)
-            kb_bank = staged.tile([F, NX, NX], F32, name="kb_bank")
-            nc.tensor.matmul(kb_bank[:], identity[:], kb_sb[:].rearrange("f b m -> f m b"), start=True, stop=True)
+            kb_by_m = kb_sb[:].rearrange("f b m -> f m b")
+            kb_mb = terms.tile([F, M_GPSIMD, NX], F32, name="kb_mb")
+            nc.scalar.activation(kb_mb[:], kb_by_m[:, 0:M_GPSIMD], COPY)
+            kb_bank = staged.tile([F, M_VECTOR, NX], F32, name="kb_bank")
+            nc.tensor.matmul(kb_bank[:], identity[:], kb_by_m[:, M_GPSIMD:NX], start=True, stop=True)
             pre_wide = terms.tile([F, PIECE // NX, NX], F32, name="pre_wide")
             nc.scalar.activation(pre_wide[:], pre_sb[:, t].unsqueeze(1).to_broadcast([F, PIECE // NX, NX]), COPY)
             return ka_sb, kb_mb, kb_bank, pre_wide
@@ -106,27 +109,27 @@ def tile_multifreqfstar_kernel(tc, x, pre, post, ka, kb, offs, out):
             pair_flipped = flipped.tile([K, HALVES, G, NX, FG], F32, name="pair_flipped")
             for half in range(HALVES):
                 a_range = slice(half * A_HALF, (half + 1) * A_HALF)
-                pair_one = work.tile([F, FLIPS, A_HALF, NX], F32, name="pair_one")
+                pair_gpsimd = work.tile([F, M_GPSIMD, A_HALF, NX], F32, name="pair_gpsimd")
                 nc.gpsimd.tensor_tensor(
-                    pair_one[:],
-                    kb_mb[:, 0:FLIPS].unsqueeze(2).to_broadcast([F, FLIPS, A_HALF, NX]),
-                    post_ka[:, 0:FLIPS, a_range].unsqueeze(3).to_broadcast([F, FLIPS, A_HALF, NX]),
+                    pair_gpsimd[:],
+                    kb_mb[:].unsqueeze(2).to_broadcast([F, M_GPSIMD, A_HALF, NX]),
+                    post_ka[:, 0:M_GPSIMD, a_range].unsqueeze(3).to_broadcast([F, M_GPSIMD, A_HALF, NX]),
                     MULT,
                 )
-                pair_three = work.tile([F, NX - FLIPS, A_HALF, NX], F32, name="pair_three")
+                pair_vector = work.tile([F, M_VECTOR, A_HALF, NX], F32, name="pair_vector")
                 nc.vector.tensor_tensor(
-                    pair_three[:],
-                    kb_bank[:, FLIPS:NX].unsqueeze(2).to_broadcast([F, NX - FLIPS, A_HALF, NX]),
-                    post_ka[:, FLIPS:NX, a_range].unsqueeze(3).to_broadcast([F, NX - FLIPS, A_HALF, NX]),
+                    pair_vector[:],
+                    kb_bank[:].unsqueeze(2).to_broadcast([F, M_VECTOR, A_HALF, NX]),
+                    post_ka[:, M_GPSIMD:NX, a_range].unsqueeze(3).to_broadcast([F, M_VECTOR, A_HALF, NX]),
                     MULT,
                 )
+                rows_of_m = [pair_gpsimd[:, m] for m in range(M_GPSIMD)] + [pair_vector[:, m] for m in range(M_VECTOR)]
                 for m in range(0, NX, FLIPS):
-                    rows = pair_one if m == 0 else pair_three[:, m - FLIPS : m]
                     flip_and_group(
                         nc,
                         flips,
                         identity,
-                        [rows[:, i].rearrange("f a b -> f (a b)") for i in range(FLIPS)],
+                        [rows_of_m[m + i].rearrange("f a b -> f (a b)") for i in range(FLIPS)],
                         pair_flipped[:, half, :, m : m + FLIPS, :],
                     )
 

@@ -13,6 +13,7 @@ NX = 16
 S = 1024
 N = NX * NX * NX
 PIECE = S
+PIECES = N // PIECE
 K = 128
 HALVES = NX * NX // K
 A_HALF = NX // HALVES
@@ -23,7 +24,6 @@ G = F // FG
 SLOTS = G // COL_TILES
 BANK = 512
 FLIPS = BANK // F
-STEPS = N // PIECE
 M_GPSIMD = 5
 M_VECTOR = NX - M_GPSIMD
 
@@ -41,9 +41,10 @@ def tile_multifreqfstar_kernel(tc, x, pre, post, ka, kb, offs, out):
     nc = tc.nc
     with (
         tc.tile_pool(name="held", bufs=1) as held,
-        tc.tile_pool(name="terms", bufs=2) as terms,
+        tc.tile_pool(name="terms", bufs=3) as terms,
         tc.tile_pool(name="work", bufs=6) as work,
         tc.tile_pool(name="flipped", bufs=2) as flipped,
+        tc.tile_pool(name="pairs_flipped", bufs=3) as pairs_flipped,
         tc.psum_pool(name="sums", bufs=1) as sums,
         tc.psum_pool(name="staged", bufs=2) as staged,
         tc.psum_pool(name="flips", bufs=5) as flips,
@@ -64,6 +65,8 @@ def tile_multifreqfstar_kernel(tc, x, pre, post, ka, kb, offs, out):
         products = sums.tile([F, SLOTS, NX * FG], F32, name="products")
         nc.tensor.matmul(products[:].rearrange("p s c -> p (s c)"), zeros[:, 0:F], zeros[:], start=True, stop=False)
 
+        x_part = [held.tile([F, S], F32, name=f"x_part{p}") for p in range(T // TERMS_OF_PART)]
+
         def stage(t):
             kb_sb = terms.tile([F, NX, NX], F32, name="kb_sb")
             ka_sb = terms.tile([F, NX, NX], F32, name="ka_sb")
@@ -80,25 +83,7 @@ def tile_multifreqfstar_kernel(tc, x, pre, post, ka, kb, offs, out):
             nc.scalar.activation(pre_wide[:], pre_sb[:, t].unsqueeze(1).to_broadcast([F, PIECE // NX, NX]), COPY)
             return ka_sb, kb_mb, kb_bank, pre_wide
 
-        def multiply(t, step, e_flipped, pair_flipped):
-            for half in range(HALVES):
-                for slot in range(step * SLOTS // STEPS, (step + 1) * SLOTS // STEPS):
-                    for j in range(COL_TILES):
-                        g = slot * COL_TILES + j
-                        nc.tensor.matmul(
-                            products[j * TILE : (j + 1) * TILE, slot, :],
-                            e_flipped[:, half, g].rearrange("k r e -> k (r e)"),
-                            pair_flipped[:, half, g].rearrange("k m e -> k e m"),
-                            start=False,
-                            stop=(t == T - 1 and half == HALVES - 1 and slot == SLOTS - 1),
-                        )
-
-        x_part = [held.tile([F, S], F32, name=f"x_part{p}") for p in range(T // TERMS_OF_PART)]
-        staged_next = stage(0)
-        flipped_before = None
-        for t in range(T):
-            ka_sb, kb_mb, kb_bank, pre_wide = staged_next
-
+        def scale_ka(t, ka_sb):
             post_ka = terms.tile([F, NX, NX], F32, name="post_ka")
             nc.vector.tensor_tensor(
                 post_ka[:],
@@ -106,59 +91,93 @@ def tile_multifreqfstar_kernel(tc, x, pre, post, ka, kb, offs, out):
                 post_sb[:, t].unsqueeze(1).to_broadcast([F, NX, NX]),
                 MULT,
             )
-            pair_flipped = flipped.tile([K, HALVES, G, NX, FG], F32, name="pair_flipped")
+            return post_ka
+
+        def build_pair(half, kb_mb, kb_bank, post_ka, pair_flipped):
+            a_range = slice(half * A_HALF, (half + 1) * A_HALF)
+            pair_gpsimd = work.tile([F, M_GPSIMD, A_HALF, NX], F32, name="pair_gpsimd")
+            nc.gpsimd.tensor_tensor(
+                pair_gpsimd[:],
+                kb_mb[:].unsqueeze(2).to_broadcast([F, M_GPSIMD, A_HALF, NX]),
+                post_ka[:, 0:M_GPSIMD, a_range].unsqueeze(3).to_broadcast([F, M_GPSIMD, A_HALF, NX]),
+                MULT,
+            )
+            pair_vector = work.tile([F, M_VECTOR, A_HALF, NX], F32, name="pair_vector")
+            nc.vector.tensor_tensor(
+                pair_vector[:],
+                kb_bank[:].unsqueeze(2).to_broadcast([F, M_VECTOR, A_HALF, NX]),
+                post_ka[:, M_GPSIMD:NX, a_range].unsqueeze(3).to_broadcast([F, M_VECTOR, A_HALF, NX]),
+                MULT,
+            )
+            rows_of_m = [pair_gpsimd[:, m] for m in range(M_GPSIMD)] + [pair_vector[:, m] for m in range(M_VECTOR)]
+            for m in range(0, NX, FLIPS):
+                flip_and_group(
+                    nc,
+                    flips,
+                    identity,
+                    [rows_of_m[m + i].rearrange("f a b -> f (a b)") for i in range(FLIPS)],
+                    pair_flipped[:, half, :, m : m + FLIPS, :],
+                )
+
+        def look_up(t, q, pre_wide, e_flipped):
+            e = work.tile([F, FLIPS, HALVES, K], F32, name="e")
+            nc.vector.tensor_tensor(
+                e[:].rearrange("f r h k -> f (r h k)"),
+                x_part[t // TERMS_OF_PART][:].indirect(offsets[:, q * (PIECE // 16) : (q + 1) * (PIECE // 16)]),
+                pre_wide[:].rearrange("f c b -> f (c b)"),
+                MULT,
+            )
             for half in range(HALVES):
-                a_range = slice(half * A_HALF, (half + 1) * A_HALF)
-                pair_gpsimd = work.tile([F, M_GPSIMD, A_HALF, NX], F32, name="pair_gpsimd")
-                nc.gpsimd.tensor_tensor(
-                    pair_gpsimd[:],
-                    kb_mb[:].unsqueeze(2).to_broadcast([F, M_GPSIMD, A_HALF, NX]),
-                    post_ka[:, 0:M_GPSIMD, a_range].unsqueeze(3).to_broadcast([F, M_GPSIMD, A_HALF, NX]),
-                    MULT,
+                flip_and_group(
+                    nc,
+                    flips,
+                    identity,
+                    [e[:, i, half, :] for i in range(FLIPS)],
+                    e_flipped[:, half, :, q * FLIPS : (q + 1) * FLIPS, :],
                 )
-                pair_vector = work.tile([F, M_VECTOR, A_HALF, NX], F32, name="pair_vector")
-                nc.vector.tensor_tensor(
-                    pair_vector[:],
-                    kb_bank[:].unsqueeze(2).to_broadcast([F, M_VECTOR, A_HALF, NX]),
-                    post_ka[:, M_GPSIMD:NX, a_range].unsqueeze(3).to_broadcast([F, M_VECTOR, A_HALF, NX]),
-                    MULT,
-                )
-                rows_of_m = [pair_gpsimd[:, m] for m in range(M_GPSIMD)] + [pair_vector[:, m] for m in range(M_VECTOR)]
-                for m in range(0, NX, FLIPS):
-                    flip_and_group(
-                        nc,
-                        flips,
-                        identity,
-                        [rows_of_m[m + i].rearrange("f a b -> f (a b)") for i in range(FLIPS)],
-                        pair_flipped[:, half, :, m : m + FLIPS, :],
-                    )
 
+        def multiply(halves, slots, e_flipped, pair_flipped, last=False):
+            for half in halves:
+                for slot in slots:
+                    for j in range(COL_TILES):
+                        g = slot * COL_TILES + j
+                        nc.tensor.matmul(
+                            products[j * TILE : (j + 1) * TILE, slot, :],
+                            e_flipped[:, half, g].rearrange("k r e -> k (r e)"),
+                            pair_flipped[:, half, g].rearrange("k m e -> k e m"),
+                            start=False,
+                            stop=(last and half == halves[-1] and slot == slots[-1]),
+                        )
+
+        def build_whole_pair(t):
+            ka_sb, kb_mb, kb_bank = staged_terms[t][0:3]
+            pair_flipped = pairs_flipped.tile([K, HALVES, G, NX, FG], F32, name="pair_flipped")
+            post_ka = scale_ka(t, ka_sb)
+            for half in both_halves:
+                build_pair(half, kb_mb, kb_bank, post_ka, pair_flipped)
+            return pair_flipped
+
+        both_halves = list(range(HALVES))
+        staged_terms = [stage(0), stage(1)]
+        pair_flipped_of = [build_whole_pair(0)]
+        e_flipped_before = None
+        for t in range(T):
+            if t + 2 < T:
+                staged_terms.append(stage(t + 2))
             if t + 1 < T:
-                staged_next = stage(t + 1)
-
+                pair_flipped_of.append(build_whole_pair(t + 1))
             e_flipped = flipped.tile([K, HALVES, G, NX, FG], F32, name="e_flipped")
-            for q in range(N // PIECE):
-                e = work.tile([F, FLIPS, HALVES, K], F32, name="e")
-                nc.vector.tensor_tensor(
-                    e[:].rearrange("f r h k -> f (r h k)"),
-                    x_part[t // TERMS_OF_PART][:].indirect(offsets[:, q * (PIECE // 16) : (q + 1) * (PIECE // 16)]),
-                    pre_wide[:].rearrange("f c b -> f (c b)"),
-                    MULT,
-                )
-                for half in range(HALVES):
-                    flip_and_group(
-                        nc,
-                        flips,
-                        identity,
-                        [e[:, i, half, :] for i in range(FLIPS)],
-                        e_flipped[:, half, :, q * FLIPS : (q + 1) * FLIPS, :],
-                    )
+            for q in range(PIECES):
+                look_up(t, q, staged_terms[t][3], e_flipped)
                 if t > 0:
-                    multiply(t - 1, q, *flipped_before)
-            flipped_before = (e_flipped, pair_flipped)
-
-        for step in range(STEPS):
-            multiply(T - 1, step, *flipped_before)
+                    multiply(
+                        both_halves,
+                        list(range(q * SLOTS // PIECES, (q + 1) * SLOTS // PIECES)),
+                        e_flipped_before,
+                        pair_flipped_of[t - 1],
+                    )
+            e_flipped_before = e_flipped
+        multiply(both_halves, list(range(SLOTS)), e_flipped_before, pair_flipped_of[T - 1], last=True)
 
         result = held.tile([F, SLOTS, FG, NX], F32, name="result")
         nc.scalar.activation(

@@ -86,27 +86,25 @@ def tile_multifreqfstar_kernel(tc, x, pre, post, ka, kb, offs, out):
         def scale_ka(t, ka_sb):
             post_ka = terms.tile([F, NX, NX], F32, name="post_ka")
             nc.vector.tensor_tensor(
-                post_ka[:],
-                ka_sb[:].rearrange("f a m -> f m a"),
-                post_sb[:, t].unsqueeze(1).to_broadcast([F, NX, NX]),
-                MULT,
+                post_ka[:], ka_sb[:], post_sb[:, t].unsqueeze(2).to_broadcast([F, NX, NX]), MULT
             )
             return post_ka
 
         def build_pair(half, kb_mb, kb_bank, post_ka, pair_flipped):
             a_range = slice(half * A_HALF, (half + 1) * A_HALF)
+            post_ka_by_m = post_ka[:].rearrange("f a m -> f m a")
             pair_gpsimd = work.tile([F, M_GPSIMD, A_HALF, NX], F32, name="pair_gpsimd")
             nc.gpsimd.tensor_tensor(
                 pair_gpsimd[:],
                 kb_mb[:].unsqueeze(2).to_broadcast([F, M_GPSIMD, A_HALF, NX]),
-                post_ka[:, 0:M_GPSIMD, a_range].unsqueeze(3).to_broadcast([F, M_GPSIMD, A_HALF, NX]),
+                post_ka_by_m[:, 0:M_GPSIMD, a_range].unsqueeze(3).to_broadcast([F, M_GPSIMD, A_HALF, NX]),
                 MULT,
             )
             pair_vector = work.tile([F, M_VECTOR, A_HALF, NX], F32, name="pair_vector")
             nc.vector.tensor_tensor(
                 pair_vector[:],
                 kb_bank[:].unsqueeze(2).to_broadcast([F, M_VECTOR, A_HALF, NX]),
-                post_ka[:, M_GPSIMD:NX, a_range].unsqueeze(3).to_broadcast([F, M_VECTOR, A_HALF, NX]),
+                post_ka_by_m[:, M_GPSIMD:NX, a_range].unsqueeze(3).to_broadcast([F, M_VECTOR, A_HALF, NX]),
                 MULT,
             )
             rows_of_m = [pair_gpsimd[:, m] for m in range(M_GPSIMD)] + [pair_vector[:, m] for m in range(M_VECTOR)]

@@ -12,10 +12,10 @@ TERMS_OF_PART = 2
 NX = 16
 S = 1024
 N = NX * NX * NX
-PIECE = S
-PIECES = N // PIECE
+AB = NX * NX
+R_PIECE = S // AB
 K = 128
-HALVES = NX * NX // K
+HALVES = AB // K
 A_HALF = NX // HALVES
 TILE = 32
 COL_TILES = F // TILE
@@ -31,7 +31,7 @@ FLOPS = T * F * N + 2 * T * F * N * NX + 2 * T * F * NX * NX * NX
 
 
 def flip_and_group(nc, flips, identity, blocks, grouped):
-    bank = flips.tile([K, FLIPS, F], F32, name="bank")
+    bank = flips.tile([K, len(blocks), F], F32, name="bank")
     for i, block in enumerate(blocks):
         nc.tensor.transpose(bank[:, i, :], block, identity[:])
     nc.scalar.activation(grouped, bank[:].rearrange("k i (g e) -> k g i e", e=FG), COPY)
@@ -41,7 +41,7 @@ def tile_multifreqfstar_kernel(tc, x, pre, post, ka, kb, offs, out):
     nc = tc.nc
     with (
         tc.tile_pool(name="held", bufs=1) as held,
-        tc.tile_pool(name="terms", bufs=3) as terms,
+        tc.tile_pool(name="in_turn", bufs=1) as in_turn,
         tc.tile_pool(name="work", bufs=6) as work,
         tc.tile_pool(name="flipped", bufs=2) as flipped,
         tc.tile_pool(name="pairs_flipped", bufs=3) as pairs_flipped,
@@ -49,80 +49,91 @@ def tile_multifreqfstar_kernel(tc, x, pre, post, ka, kb, offs, out):
         tc.psum_pool(name="staged", bufs=2) as staged,
         tc.psum_pool(name="flips", bufs=5) as flips,
     ):
+        x_part = [held.tile([F, S], F32, name=f"x_part{p}") for p in range(T // TERMS_OF_PART)]
+        kb_sb = [held.tile([F, NX, NX], F32, name=f"kb_sb{t}") for t in range(T)]
+        ka_sb = [held.tile([F, NX, NX], F32, name=f"ka_sb{t}") for t in range(T)]
+        scales_wide = [held.tile([F, R_PIECE, AB], F32, name=f"scales_wide{t}") for t in range(T)]
+        scales = held.tile([F, T, NX, NX], F32, name="scales")
         offsets = held.tile([F, N // 16], U16, name="offsets")
-        nc.sync.dma_start(offsets[:], offs)
+
+        def load_kernels(t):
+            nc.sync.dma_start(kb_sb[t][:], kb[t * F : (t + 1) * F, :].rearrange("f (b m) -> f b m", m=NX))
+            nc.sync.dma_start(ka_sb[t][:], ka[t * F : (t + 1) * F, :].rearrange("f (a m) -> f a m", m=NX))
+
+        def load_part(p):
+            nc.sync.dma_start(x_part[p][:], x[p * F : (p + 1) * F, :])
+
+        def make_scales(t):
+            for a in range(NX):
+                nc.scalar.activation(scales[:, t, a], pre_sb[:, t], COPY, scale=post_sb[:, t, a : a + 1])
+            nc.sync.dma_start(
+                scales_wide[t][:],
+                scales[:, t].rearrange("f a b -> f (a b)").unsqueeze(1).to_broadcast([F, R_PIECE, AB]),
+            )
 
         pre_sb = held.tile([F, T, NX], F32, name="pre_sb")
         post_sb = held.tile([F, T, NX], F32, name="post_sb")
         nc.scalar.dma_start(pre_sb[:], pre.rearrange("(t f) b -> f t b", f=F))
         nc.scalar.dma_start(post_sb[:], post.rearrange("(t f) a -> f t a", f=F))
+        load_kernels(0)
+        load_kernels(1)
+        nc.sync.dma_start(offsets[:], offs)
+        load_part(0)
 
         identity = held.tile([F, F], F32, name="identity")
         make_identity(nc, identity[:])
 
-        zeros = held.tile([K, BANK], F32, name="zeros")
-        nc.gpsimd.memset(zeros[:], 0.0)
-        products = sums.tile([F, SLOTS, NX * FG], F32, name="products")
-        nc.tensor.matmul(products[:].rearrange("p s c -> p (s c)"), zeros[:, 0:F], zeros[:], start=True, stop=False)
+        products = sums.tile([F, SLOTS, FG * NX], F32, name="products")
 
-        x_part = [held.tile([F, S], F32, name=f"x_part{p}") for p in range(T // TERMS_OF_PART)]
-
-        def stage(t):
-            kb_sb = terms.tile([F, NX, NX], F32, name="kb_sb")
-            ka_sb = terms.tile([F, NX, NX], F32, name="ka_sb")
-            nc.sync.dma_start(kb_sb[:], kb[t * F : (t + 1) * F, :].rearrange("f (b m) -> f b m", m=NX))
-            nc.sync.dma_start(ka_sb[:], ka[t * F : (t + 1) * F, :].rearrange("f (a m) -> f a m", m=NX))
-            if t % TERMS_OF_PART == 0:
-                nc.sync.dma_start(x_part[t // TERMS_OF_PART][:], x[(t // TERMS_OF_PART) * F : (t // TERMS_OF_PART + 1) * F, :])
-            kb_by_m = kb_sb[:].rearrange("f b m -> f m b")
-            kb_mb = terms.tile([F, M_GPSIMD, NX], F32, name="kb_mb")
-            nc.scalar.activation(kb_mb[:], kb_by_m[:, 0:M_GPSIMD], COPY)
+        def stage_kb(t):
             kb_bank = staged.tile([F, M_VECTOR, NX], F32, name="kb_bank")
-            nc.tensor.matmul(kb_bank[:], identity[:], kb_by_m[:, M_GPSIMD:NX], start=True, stop=True)
-            pre_wide = terms.tile([F, PIECE // NX, NX], F32, name="pre_wide")
-            nc.scalar.activation(pre_wide[:], pre_sb[:, t].unsqueeze(1).to_broadcast([F, PIECE // NX, NX]), COPY)
-            return ka_sb, kb_mb, kb_bank, pre_wide
+            nc.tensor.matmul(
+                kb_bank[:], identity[:], kb_sb[t][:].rearrange("f b m -> f m b")[:, 0:M_VECTOR], start=True, stop=True
+            )
+            return kb_bank
 
-        def scale_ka(t, ka_sb):
-            post_ka = terms.tile([F, NX, NX], F32, name="post_ka")
-            nc.vector.tensor_tensor(
-                post_ka[:], ka_sb[:], post_sb[:, t].unsqueeze(2).to_broadcast([F, NX, NX]), MULT
-            )
-            return post_ka
-
-        def build_pair(half, kb_mb, kb_bank, post_ka, pair_flipped):
-            a_range = slice(half * A_HALF, (half + 1) * A_HALF)
-            post_ka_by_m = post_ka[:].rearrange("f a m -> f m a")
-            pair_gpsimd = work.tile([F, M_GPSIMD, A_HALF, NX], F32, name="pair_gpsimd")
-            nc.gpsimd.tensor_tensor(
-                pair_gpsimd[:],
-                kb_mb[:].unsqueeze(2).to_broadcast([F, M_GPSIMD, A_HALF, NX]),
-                post_ka_by_m[:, 0:M_GPSIMD, a_range].unsqueeze(3).to_broadcast([F, M_GPSIMD, A_HALF, NX]),
-                MULT,
-            )
-            pair_vector = work.tile([F, M_VECTOR, A_HALF, NX], F32, name="pair_vector")
-            nc.vector.tensor_tensor(
-                pair_vector[:],
-                kb_bank[:].unsqueeze(2).to_broadcast([F, M_VECTOR, A_HALF, NX]),
-                post_ka_by_m[:, M_GPSIMD:NX, a_range].unsqueeze(3).to_broadcast([F, M_VECTOR, A_HALF, NX]),
-                MULT,
-            )
-            rows_of_m = [pair_gpsimd[:, m] for m in range(M_GPSIMD)] + [pair_vector[:, m] for m in range(M_VECTOR)]
-            for m in range(0, NX, FLIPS):
-                flip_and_group(
-                    nc,
-                    flips,
-                    identity,
-                    [rows_of_m[m + i].rearrange("f a b -> f (a b)") for i in range(FLIPS)],
-                    pair_flipped[:, half, :, m : m + FLIPS, :],
+        def build_pair(t, kb_bank):
+            pair_flipped = pairs_flipped.tile([K, HALVES, G, NX, FG], F32, name="pair_flipped")
+            kb_by_m = kb_sb[t][:].rearrange("f b m -> f m b")
+            ka_by_m = ka_sb[t][:].rearrange("f a m -> f m a")
+            kb_gpsimd = in_turn.tile([F, M_GPSIMD, NX], F32, name="kb_gpsimd")
+            nc.vector.tensor_copy(kb_gpsimd[:], kb_by_m[:, NX - M_GPSIMD : NX])
+            for half in range(HALVES):
+                a_range = slice(half * A_HALF, (half + 1) * A_HALF)
+                pair_gpsimd = work.tile([F, M_GPSIMD, A_HALF, NX], F32, name="pair_gpsimd")
+                nc.gpsimd.tensor_tensor(
+                    pair_gpsimd[:],
+                    kb_gpsimd[:].unsqueeze(2).to_broadcast([F, M_GPSIMD, A_HALF, NX]),
+                    ka_by_m[:, NX - M_GPSIMD : NX, a_range].unsqueeze(3).to_broadcast([F, M_GPSIMD, A_HALF, NX]),
+                    MULT,
                 )
+                pair_vector = work.tile([F, M_VECTOR, A_HALF, NX], F32, name="pair_vector")
+                nc.vector.tensor_tensor(
+                    pair_vector[:],
+                    kb_bank[:].unsqueeze(2).to_broadcast([F, M_VECTOR, A_HALF, NX]),
+                    ka_by_m[:, 0:M_VECTOR, a_range].unsqueeze(3).to_broadcast([F, M_VECTOR, A_HALF, NX]),
+                    MULT,
+                )
+                rows_of_m = (
+                    [pair_vector[:, m] for m in range(M_VECTOR)]
+                    + [pair_gpsimd[:, m] for m in range(M_GPSIMD)]
+                )
+                for m in range(0, NX, FLIPS):
+                    flip_and_group(
+                        nc,
+                        flips,
+                        identity,
+                        [rows_of_m[m + i].rearrange("f a b -> f (a b)") for i in range(FLIPS)],
+                        pair_flipped[:, half, :, m : m + FLIPS, :],
+                    )
+            return pair_flipped
 
-        def look_up(t, q, pre_wide, e_flipped):
-            e = work.tile([F, FLIPS, HALVES, K], F32, name="e")
+        def look_up(t, r0, n_r, e_flipped):
+            e_post = work.tile([F, n_r, HALVES, K], F32, name="e_post")
             nc.vector.tensor_tensor(
-                e[:].rearrange("f r h k -> f (r h k)"),
-                x_part[t // TERMS_OF_PART][:].indirect(offsets[:, q * (PIECE // 16) : (q + 1) * (PIECE // 16)]),
-                pre_wide[:].rearrange("f c b -> f (c b)"),
+                e_post[:].rearrange("f r h k -> f (r h k)"),
+                x_part[t // TERMS_OF_PART][:].indirect(offsets[:, r0 * AB // 16 : (r0 + n_r) * AB // 16]),
+                scales_wide[t][:, 0:n_r].rearrange("f r k -> f (r k)"),
                 MULT,
             )
             for half in range(HALVES):
@@ -130,52 +141,48 @@ def tile_multifreqfstar_kernel(tc, x, pre, post, ka, kb, offs, out):
                     nc,
                     flips,
                     identity,
-                    [e[:, i, half, :] for i in range(FLIPS)],
-                    e_flipped[:, half, :, q * FLIPS : (q + 1) * FLIPS, :],
+                    [e_post[:, i, half, :] for i in range(n_r)],
+                    e_flipped[:, half, :, r0 : r0 + n_r, :],
                 )
 
-        def multiply(halves, slots, e_flipped, pair_flipped, last=False):
-            for half in halves:
-                for slot in slots:
+        def multiply(t, slots, e_flipped, pair_flipped):
+            for half in range(HALVES):
+                for s in slots:
                     for j in range(COL_TILES):
-                        g = slot * COL_TILES + j
+                        g = s * COL_TILES + j
                         nc.tensor.matmul(
-                            products[j * TILE : (j + 1) * TILE, slot, :],
+                            products[j * TILE : (j + 1) * TILE, s, :],
                             e_flipped[:, half, g].rearrange("k r e -> k (r e)"),
                             pair_flipped[:, half, g].rearrange("k m e -> k e m"),
-                            start=False,
-                            stop=(last and half == halves[-1] and slot == slots[-1]),
+                            start=(t == 0 and half == 0 and s == 0),
+                            stop=(t == T - 1 and half == HALVES - 1 and s == SLOTS - 1),
                         )
 
-        def build_whole_pair(t):
-            ka_sb, kb_mb, kb_bank = staged_terms[t][0:3]
-            pair_flipped = pairs_flipped.tile([K, HALVES, G, NX, FG], F32, name="pair_flipped")
-            post_ka = scale_ka(t, ka_sb)
-            for half in both_halves:
-                build_pair(half, kb_mb, kb_bank, post_ka, pair_flipped)
-            return pair_flipped
-
-        both_halves = list(range(HALVES))
-        staged_terms = [stage(0), stage(1)]
-        pair_flipped_of = [build_whole_pair(0)]
+        kb_banks = [stage_kb(0), stage_kb(1)]
+        make_scales(0)
+        pair_flipped_of = [build_pair(0, kb_banks[0])]
+        load_part(1)
+        for t in range(2, T):
+            load_kernels(t)
+        for t in range(1, T):
+            make_scales(t)
         e_flipped_before = None
         for t in range(T):
             if t + 2 < T:
-                staged_terms.append(stage(t + 2))
+                kb_banks.append(stage_kb(t + 2))
             if t + 1 < T:
-                pair_flipped_of.append(build_whole_pair(t + 1))
+                pair_flipped_of.append(build_pair(t + 1, kb_banks[t + 1]))
             e_flipped = flipped.tile([K, HALVES, G, NX, FG], F32, name="e_flipped")
-            for q in range(PIECES):
-                look_up(t, q, staged_terms[t][3], e_flipped)
+            for r0 in range(0, NX, R_PIECE):
+                if t == T - 1 and r0 + R_PIECE == NX:
+                    look_up(t, r0, R_PIECE // 2, e_flipped)
+                    look_up(t, r0 + R_PIECE // 2, R_PIECE // 2, e_flipped)
+                else:
+                    look_up(t, r0, R_PIECE, e_flipped)
                 if t > 0:
-                    multiply(
-                        both_halves,
-                        list(range(q * SLOTS // PIECES, (q + 1) * SLOTS // PIECES)),
-                        e_flipped_before,
-                        pair_flipped_of[t - 1],
-                    )
+                    multiply(t - 1, range(r0 * SLOTS // NX, (r0 + R_PIECE) * SLOTS // NX), e_flipped_before, pair_flipped_of[t - 1])
             e_flipped_before = e_flipped
-        multiply(both_halves, list(range(SLOTS)), e_flipped_before, pair_flipped_of[T - 1], last=True)
+        multiply(T - 1, range(SLOTS), e_flipped_before, pair_flipped_of[T - 1])
 
         result = held.tile([F, SLOTS, FG, NX], F32, name="result")
         nc.scalar.activation(
@@ -185,6 +192,6 @@ def tile_multifreqfstar_kernel(tc, x, pre, post, ka, kb, offs, out):
         out_rows = out.rearrange("(s j e) (r m) -> j e r s m", j=COL_TILES, e=FG, m=NX)
         result_rows = result[:].rearrange("(j r e) s c m -> j e r s c m", j=COL_TILES, e=FG)
         for j in range(COL_TILES):
-            for f in range(FG):
-                queue = nc.sync if f % 2 == 0 else nc.scalar
-                queue.dma_start(out_rows[j, f], result_rows[j, f, :, :, f, :])
+            for e in range(FG):
+                queue = nc.sync if e % 2 == 0 else nc.scalar
+                queue.dma_start(out_rows[j, e], result_rows[j, e, :, :, e, :])

@@ -41,7 +41,7 @@ def tile_multifreqfstar_kernel(tc, x, pre, post, ka, kb, offs, out):
     nc = tc.nc
     with (
         tc.tile_pool(name="held", bufs=1) as held,
-        tc.tile_pool(name="in_turn", bufs=1) as in_turn,
+        tc.tile_pool(name="in_turn", bufs=2) as in_turn,
         tc.tile_pool(name="work", bufs=6) as work,
         tc.tile_pool(name="flipped", bufs=2) as flipped,
         tc.tile_pool(name="pairs_flipped", bufs=3) as pairs_flipped,
@@ -92,12 +92,23 @@ def tile_multifreqfstar_kernel(tc, x, pre, post, ka, kb, offs, out):
             )
             return kb_bank
 
-        def build_pair(t, kb_bank):
+        def vector_share(pair_vector, kb_of_m, ka_of_m, m0, m1):
+            nc.vector.tensor_tensor(
+                pair_vector[:, m0:m1],
+                kb_of_m[:, m0:m1].unsqueeze(2).to_broadcast([F, m1 - m0, A_HALF, NX]),
+                ka_of_m[:, m0:m1].unsqueeze(3).to_broadcast([F, m1 - m0, A_HALF, NX]),
+                MULT,
+            )
+
+        def stage_kb_gpsimd(t):
+            kb_gpsimd = in_turn.tile([F, M_GPSIMD, NX], F32, name="kb_gpsimd")
+            nc.vector.tensor_copy(kb_gpsimd[:], kb_sb[t][:].rearrange("f b m -> f m b")[:, NX - M_GPSIMD : NX])
+            return kb_gpsimd
+
+        def build_pair(t, kb_bank, kb_gpsimd):
             pair_flipped = pairs_flipped.tile([K, HALVES, G, NX, FG], F32, name="pair_flipped")
             kb_by_m = kb_sb[t][:].rearrange("f b m -> f m b")
             ka_by_m = ka_sb[t][:].rearrange("f a m -> f m a")
-            kb_gpsimd = in_turn.tile([F, M_GPSIMD, NX], F32, name="kb_gpsimd")
-            nc.vector.tensor_copy(kb_gpsimd[:], kb_by_m[:, NX - M_GPSIMD : NX])
             for half in range(HALVES):
                 a_range = slice(half * A_HALF, (half + 1) * A_HALF)
                 pair_gpsimd = work.tile([F, M_GPSIMD, A_HALF, NX], F32, name="pair_gpsimd")
@@ -108,12 +119,10 @@ def tile_multifreqfstar_kernel(tc, x, pre, post, ka, kb, offs, out):
                     MULT,
                 )
                 pair_vector = work.tile([F, M_VECTOR, A_HALF, NX], F32, name="pair_vector")
-                nc.vector.tensor_tensor(
-                    pair_vector[:],
-                    kb_bank[:].unsqueeze(2).to_broadcast([F, M_VECTOR, A_HALF, NX]),
-                    ka_by_m[:, 0:M_VECTOR, a_range].unsqueeze(3).to_broadcast([F, M_VECTOR, A_HALF, NX]),
-                    MULT,
-                )
+                from_sbuf = FLIPS if t == 0 and half == 0 else 0
+                if from_sbuf:
+                    vector_share(pair_vector, kb_by_m, ka_by_m[:, :, a_range], 0, from_sbuf)
+                vector_share(pair_vector, kb_bank, ka_by_m[:, :, a_range], from_sbuf, M_VECTOR)
                 rows_of_m = (
                     [pair_vector[:, m] for m in range(M_VECTOR)]
                     + [pair_gpsimd[:, m] for m in range(M_GPSIMD)]
@@ -159,8 +168,9 @@ def tile_multifreqfstar_kernel(tc, x, pre, post, ka, kb, offs, out):
                         )
 
         kb_banks = [stage_kb(0), stage_kb(1)]
+        kb_gpsimds = [stage_kb_gpsimd(0), stage_kb_gpsimd(1)]
         make_scales(0)
-        pair_flipped_of = [build_pair(0, kb_banks[0])]
+        pair_flipped_of = [build_pair(0, kb_banks[0], kb_gpsimds[0])]
         load_part(1)
         for t in range(2, T):
             load_kernels(t)
@@ -171,9 +181,11 @@ def tile_multifreqfstar_kernel(tc, x, pre, post, ka, kb, offs, out):
             if t + 2 < T:
                 kb_banks.append(stage_kb(t + 2))
             if t + 1 < T:
-                pair_flipped_of.append(build_pair(t + 1, kb_banks[t + 1]))
+                pair_flipped_of.append(build_pair(t + 1, kb_banks[t + 1], kb_gpsimds[t + 1]))
             e_flipped = flipped.tile([K, HALVES, G, NX, FG], F32, name="e_flipped")
             for r0 in range(0, NX, R_PIECE):
+                if r0 + R_PIECE == NX and t + 2 < T:
+                    kb_gpsimds.append(stage_kb_gpsimd(t + 2))
                 if t == T - 1 and r0 + R_PIECE == NX:
                     look_up(t, r0, R_PIECE // 2, e_flipped)
                     look_up(t, r0 + R_PIECE // 2, R_PIECE // 2, e_flipped)

@@ -22,6 +22,8 @@ COL_TILES = F // TILE
 FG = TILE // NX
 G = F // FG
 SLOTS = G // COL_TILES
+PRODUCT_BANKS = 2
+BANK_SLOTS = SLOTS // PRODUCT_BANKS
 BANK = 512
 FLIPS = BANK // F
 M_GPSIMD = 5
@@ -47,7 +49,7 @@ def tile_multifreqfstar_kernel(tc, x, pre, post, ka, kb, offs, out):
         tc.tile_pool(name="pairs_flipped", bufs=3) as pairs_flipped,
         tc.psum_pool(name="sums", bufs=1) as sums,
         tc.psum_pool(name="staged", bufs=2) as staged,
-        tc.psum_pool(name="flips", bufs=5) as flips,
+        tc.psum_pool(name="flips", bufs=4) as flips,
     ):
         x_part = [held.tile([F, S], F32, name=f"x_part{p}") for p in range(T // TERMS_OF_PART)]
         kb_sb = [held.tile([F, NX, NX], F32, name=f"kb_sb{t}") for t in range(T)]
@@ -56,9 +58,9 @@ def tile_multifreqfstar_kernel(tc, x, pre, post, ka, kb, offs, out):
         scales = held.tile([F, T, NX, NX], F32, name="scales")
         offsets = held.tile([F, N // 16], U16, name="offsets")
 
-        def load_kernels(t):
+        def load_kernels(t, ka_queue):
             nc.sync.dma_start(kb_sb[t][:], kb[t * F : (t + 1) * F, :].rearrange("f (b m) -> f b m", m=NX))
-            nc.sync.dma_start(ka_sb[t][:], ka[t * F : (t + 1) * F, :].rearrange("f (a m) -> f a m", m=NX))
+            ka_queue.dma_start(ka_sb[t][:], ka[t * F : (t + 1) * F, :].rearrange("f (a m) -> f a m", m=NX))
 
         def load_part(p):
             nc.sync.dma_start(x_part[p][:], x[p * F : (p + 1) * F, :])
@@ -73,17 +75,17 @@ def tile_multifreqfstar_kernel(tc, x, pre, post, ka, kb, offs, out):
 
         pre_sb = held.tile([F, T, NX], F32, name="pre_sb")
         post_sb = held.tile([F, T, NX], F32, name="post_sb")
+        load_kernels(0, nc.scalar)
         nc.scalar.dma_start(pre_sb[:], pre.rearrange("(t f) b -> f t b", f=F))
         nc.scalar.dma_start(post_sb[:], post.rearrange("(t f) a -> f t a", f=F))
-        load_kernels(0)
-        load_kernels(1)
+        load_kernels(1, nc.sync)
         nc.sync.dma_start(offsets[:], offs)
         load_part(0)
 
         identity = held.tile([F, F], F32, name="identity")
         make_identity(nc, identity[:])
 
-        products = sums.tile([F, SLOTS, FG * NX], F32, name="products")
+        products = [sums.tile([F, BANK_SLOTS, FG * NX], F32, name=f"products{b}") for b in range(PRODUCT_BANKS)]
 
         def stage_kb(t):
             kb_bank = staged.tile([F, M_VECTOR, NX], F32, name="kb_bank")
@@ -102,7 +104,14 @@ def tile_multifreqfstar_kernel(tc, x, pre, post, ka, kb, offs, out):
 
         def stage_kb_gpsimd(t):
             kb_gpsimd = in_turn.tile([F, M_GPSIMD, NX], F32, name="kb_gpsimd")
-            nc.vector.tensor_copy(kb_gpsimd[:], kb_sb[t][:].rearrange("f b m -> f m b")[:, NX - M_GPSIMD : NX])
+            kb_share = kb_sb[t][:].rearrange("f b m -> f m b")[:, NX - M_GPSIMD : NX]
+            if t == 0:
+                nc.vector.tensor_copy(kb_gpsimd[:], kb_share)
+            elif t == 1:
+                nc.scalar.activation(kb_gpsimd[:], kb_share, COPY)
+            else:
+                nc.scalar.activation(kb_gpsimd[:, 1:M_GPSIMD], kb_share[:, 1:M_GPSIMD], COPY)
+                nc.vector.tensor_copy(kb_gpsimd[:, 0:1], kb_share[:, 0:1])
             return kb_gpsimd
 
         def build_pair(t, kb_bank, kb_gpsimd):
@@ -160,11 +169,11 @@ def tile_multifreqfstar_kernel(tc, x, pre, post, ka, kb, offs, out):
                     for j in range(COL_TILES):
                         g = s * COL_TILES + j
                         nc.tensor.matmul(
-                            products[j * TILE : (j + 1) * TILE, s, :],
+                            products[s // BANK_SLOTS][j * TILE : (j + 1) * TILE, s % BANK_SLOTS, :],
                             e_flipped[:, half, g].rearrange("k r e -> k (r e)"),
                             pair_flipped[:, half, g].rearrange("k m e -> k e m"),
-                            start=(t == 0 and half == 0 and s == 0),
-                            stop=(t == T - 1 and half == HALVES - 1 and s == SLOTS - 1),
+                            start=(t == 0 and half == 0 and s % BANK_SLOTS == 0),
+                            stop=(t == T - 1 and half == HALVES - 1 and s % BANK_SLOTS == BANK_SLOTS - 1),
                         )
 
         kb_banks = [stage_kb(0), stage_kb(1)]
@@ -173,7 +182,7 @@ def tile_multifreqfstar_kernel(tc, x, pre, post, ka, kb, offs, out):
         pair_flipped_of = [build_pair(0, kb_banks[0], kb_gpsimds[0])]
         load_part(1)
         for t in range(2, T):
-            load_kernels(t)
+            load_kernels(t, nc.sync)
         for t in range(1, T):
             make_scales(t)
         e_flipped_before = None
@@ -194,12 +203,11 @@ def tile_multifreqfstar_kernel(tc, x, pre, post, ka, kb, offs, out):
                 if t > 0:
                     multiply(t - 1, range(r0 * SLOTS // NX, (r0 + R_PIECE) * SLOTS // NX), e_flipped_before, pair_flipped_of[t - 1])
             e_flipped_before = e_flipped
-        multiply(T - 1, range(SLOTS), e_flipped_before, pair_flipped_of[T - 1])
-
         result = held.tile([F, SLOTS, FG, NX], F32, name="result")
-        nc.scalar.activation(
-            result[:].rearrange("p s e m -> p (s e m)"), products[:].rearrange("p s c -> p (s c)"), COPY
-        )
+        for b in range(PRODUCT_BANKS):
+            slots = slice(b * BANK_SLOTS, (b + 1) * BANK_SLOTS)
+            multiply(T - 1, range(slots.start, slots.stop), e_flipped_before, pair_flipped_of[T - 1])
+            nc.scalar.activation(result[:, slots].rearrange("p s e m -> p s (e m)"), products[b][:], COPY)
 
         out_rows = out.rearrange("(s j e) (r m) -> j e r s m", j=COL_TILES, e=FG, m=NX)
         result_rows = result[:].rearrange("(j r e) s c m -> j e r s c m", j=COL_TILES, e=FG)

@@ -118,32 +118,36 @@ def tile_multifreqfstar_kernel(tc, x, pre, post, ka, kb, offs, out):
             pair_flipped = pairs_flipped.tile([K, HALVES, G, NX, FG], F32, name="pair_flipped")
             kb_by_m = kb_sb[t][:].rearrange("f b m -> f m b")
             ka_by_m = ka_sb[t][:].rearrange("f a m -> f m a")
+            pair_gpsimd = work.tile([F, M_GPSIMD, NX, NX], F32, name="pair_gpsimd")
+            nc.gpsimd.tensor_tensor(
+                pair_gpsimd[:],
+                kb_gpsimd[:].unsqueeze(2).to_broadcast([F, M_GPSIMD, NX, NX]),
+                ka_by_m[:, NX - M_GPSIMD : NX].unsqueeze(3).to_broadcast([F, M_GPSIMD, NX, NX]),
+                MULT,
+            )
+            rows_of = []
             for half in range(HALVES):
                 a_range = slice(half * A_HALF, (half + 1) * A_HALF)
-                pair_gpsimd = work.tile([F, M_GPSIMD, A_HALF, NX], F32, name="pair_gpsimd")
-                nc.gpsimd.tensor_tensor(
-                    pair_gpsimd[:],
-                    kb_gpsimd[:].unsqueeze(2).to_broadcast([F, M_GPSIMD, A_HALF, NX]),
-                    ka_by_m[:, NX - M_GPSIMD : NX, a_range].unsqueeze(3).to_broadcast([F, M_GPSIMD, A_HALF, NX]),
-                    MULT,
-                )
                 pair_vector = work.tile([F, M_VECTOR, A_HALF, NX], F32, name="pair_vector")
                 from_sbuf = FLIPS if t == 0 and half == 0 else 0
                 if from_sbuf:
                     vector_share(pair_vector, kb_by_m, ka_by_m[:, :, a_range], 0, from_sbuf)
                 vector_share(pair_vector, kb_bank, ka_by_m[:, :, a_range], from_sbuf, M_VECTOR)
-                rows_of_m = (
-                    [pair_vector[:, m] for m in range(M_VECTOR)]
-                    + [pair_gpsimd[:, m] for m in range(M_GPSIMD)]
+                rows_of.append(
+                    [pair_vector[:, m] for m in range(M_VECTOR)] + [pair_gpsimd[:, m, a_range] for m in range(M_GPSIMD)]
                 )
-                for m in range(0, NX, FLIPS):
-                    flip_and_group(
-                        nc,
-                        flips,
-                        identity,
-                        [rows_of_m[m + i].rearrange("f a b -> f (a b)") for i in range(FLIPS)],
-                        pair_flipped[:, half, :, m : m + FLIPS, :],
-                    )
+            all_vector = range(0, M_VECTOR // FLIPS * FLIPS, FLIPS)
+            with_gpsimd = range(M_VECTOR // FLIPS * FLIPS, NX, FLIPS)
+            for ms in (all_vector, with_gpsimd):
+                for half in range(HALVES):
+                    for m in ms:
+                        flip_and_group(
+                            nc,
+                            flips,
+                            identity,
+                            [rows_of[half][m + i].rearrange("f a b -> f (a b)") for i in range(FLIPS)],
+                            pair_flipped[:, half, :, m : m + FLIPS, :],
+                        )
             return pair_flipped
 
         def look_up(t, r0, n_r, e_flipped):

@@ -36,7 +36,7 @@ def flip_and_group(nc, flips, identity, blocks, grouped):
     bank = flips.tile([K, len(blocks), F], F32, name="bank")
     for i, block in enumerate(blocks):
         nc.tensor.transpose(bank[:, i, :], block, identity[:])
-    nc.scalar.activation(grouped, bank[:].rearrange("k i (g e) -> k g i e", e=FG), COPY)
+    nc.scalar.activation(grouped, bank[:].rearrange("k i (e g) -> k g i e", e=FG), COPY)
 
 
 def tile_multifreqfstar_kernel(tc, x, pre, post, ka, kb, offs, out):
@@ -207,15 +207,13 @@ def tile_multifreqfstar_kernel(tc, x, pre, post, ka, kb, offs, out):
                 if t > 0:
                     multiply(t - 1, range(r0 * SLOTS // NX, (r0 + R_PIECE) * SLOTS // NX), e_flipped_before, pair_flipped_of[t - 1])
             e_flipped_before = e_flipped
-        result = held.tile([F, SLOTS, FG, NX], F32, name="result")
+        out_rows = out.rearrange("(e s j) c -> e s (j c)", e=FG, j=COL_TILES).rearrange("e s (q m) -> e q s m", m=NX)
         for b in range(PRODUCT_BANKS):
             slots = slice(b * BANK_SLOTS, (b + 1) * BANK_SLOTS)
             multiply(T - 1, range(slots.start, slots.stop), e_flipped_before, pair_flipped_of[T - 1])
-            nc.scalar.activation(result[:, slots].rearrange("p s e m -> p s (e m)"), products[b][:], COPY)
-
-        out_rows = out.rearrange("(s j e) (r m) -> j e r s m", j=COL_TILES, e=FG, m=NX)
-        result_rows = result[:].rearrange("(j r e) s c m -> j e r s c m", j=COL_TILES, e=FG)
-        for j in range(COL_TILES):
+            result = held.tile([F, BANK_SLOTS, FG, NX], F32, name=f"result{b}")
+            nc.scalar.activation(result[:].rearrange("p s e m -> p s (e m)"), products[b][:], COPY)
+            result_rows = result[:].rearrange("(q e) s c m -> e q s c m", e=FG)
             for e in range(FG):
                 queue = nc.sync if e % 2 == 0 else nc.scalar
-                queue.dma_start(out_rows[j, e], result_rows[j, e, :, :, e, :])
+                queue.dma_start(out_rows[e, :, slots, :], result_rows[e, :, :, e, :])

import concourse.mybir as mybir
from concourse.masks import make_identity

F32 = mybir.dt.float32
U16 = mybir.dt.uint16
MULT = mybir.AluOpType.mult
COPY = mybir.ActivationFunctionType.Copy

F = 128
T = 4
TERMS_OF_PART = 2
NX = 16
S = 1024
N = NX * NX * NX
AB = NX * NX
R_PIECE = S // AB
K = 128
HALVES = AB // K
A_HALF = NX // HALVES
TILE = 32
COL_TILES = F // TILE
FG = TILE // NX
G = F // FG
SLOTS = G // COL_TILES
PRODUCT_BANKS = 2
BANK_SLOTS = SLOTS // PRODUCT_BANKS
BANK = 512
FLIPS = BANK // F
M_GPSIMD = 5
M_VECTOR = NX - M_GPSIMD

FLOPS = T * F * N + 2 * T * F * N * NX + 2 * T * F * NX * NX * NX


def flip_and_group(nc, flips, identity, blocks, grouped):
    bank = flips.tile([K, len(blocks), F], F32, name="bank")
    for i, block in enumerate(blocks):
        nc.tensor.transpose(bank[:, i, :], block, identity[:])
    nc.scalar.activation(grouped, bank[:].rearrange("k i (e g) -> k g i e", e=FG), COPY)


def tile_multifreqfstar_kernel(tc, x, pre, post, ka, kb, offs, out):
    nc = tc.nc
    with (
        tc.tile_pool(name="held", bufs=1) as held,
        tc.tile_pool(name="in_turn", bufs=2) as in_turn,
        tc.tile_pool(name="work", bufs=6) as work,
        tc.tile_pool(name="flipped", bufs=2) as flipped,
        tc.tile_pool(name="pairs_flipped", bufs=3) as pairs_flipped,
        tc.psum_pool(name="sums", bufs=1) as sums,
        tc.psum_pool(name="staged", bufs=2) as staged,
        tc.psum_pool(name="flips", bufs=4) as flips,
    ):
        x_part = [held.tile([F, S], F32, name=f"x_part{p}") for p in range(T // TERMS_OF_PART)]
        kb_sb = [held.tile([F, NX, NX], F32, name=f"kb_sb{t}") for t in range(T)]
        ka_sb = [held.tile([F, NX, NX], F32, name=f"ka_sb{t}") for t in range(T)]
        scales_wide = [held.tile([F, R_PIECE, AB], F32, name=f"scales_wide{t}") for t in range(T)]
        scales = held.tile([F, T, NX, NX], F32, name="scales")
        offsets = held.tile([F, N // 16], U16, name="offsets")

        def load_kernels(t, ka_queue):
            nc.sync.dma_start(kb_sb[t][:], kb[t * F : (t + 1) * F, :].rearrange("f (b m) -> f b m", m=NX))
            ka_queue.dma_start(ka_sb[t][:], ka[t * F : (t + 1) * F, :].rearrange("f (a m) -> f a m", m=NX))

        def load_part(p):
            nc.sync.dma_start(x_part[p][:], x[p * F : (p + 1) * F, :])

        def make_scales(t):
            for a in range(NX):
                nc.scalar.activation(scales[:, t, a], pre_sb[:, t], COPY, scale=post_sb[:, t, a : a + 1])
            nc.sync.dma_start(
                scales_wide[t][:],
                scales[:, t].rearrange("f a b -> f (a b)").unsqueeze(1).to_broadcast([F, R_PIECE, AB]),
            )

        pre_sb = held.tile([F, T, NX], F32, name="pre_sb")
        post_sb = held.tile([F, T, NX], F32, name="post_sb")
        load_kernels(0, nc.scalar)
        nc.scalar.dma_start(pre_sb[:], pre.rearrange("(t f) b -> f t b", f=F))
        nc.scalar.dma_start(post_sb[:], post.rearrange("(t f) a -> f t a", f=F))
        load_kernels(1, nc.sync)
        nc.sync.dma_start(offsets[:], offs)
        load_part(0)

        identity = held.tile([F, F], F32, name="identity")
        make_identity(nc, identity[:])

        products = [sums.tile([F, BANK_SLOTS, FG * NX], F32, name=f"products{b}") for b in range(PRODUCT_BANKS)]

        def stage_kb(t):
            kb_bank = staged.tile([F, M_VECTOR, NX], F32, name="kb_bank")
            nc.tensor.matmul(
                kb_bank[:], identity[:], kb_sb[t][:].rearrange("f b m -> f m b")[:, 0:M_VECTOR], start=True, stop=True
            )
            return kb_bank

        def vector_share(pair_vector, kb_of_m, ka_of_m, m0, m1):
            nc.vector.tensor_tensor(
                pair_vector[:, m0:m1],
                kb_of_m[:, m0:m1].unsqueeze(2).to_broadcast([F, m1 - m0, A_HALF, NX]),
                ka_of_m[:, m0:m1].unsqueeze(3).to_broadcast([F, m1 - m0, A_HALF, NX]),
                MULT,
            )

        def stage_kb_gpsimd(t):
            kb_gpsimd = in_turn.tile([F, M_GPSIMD, NX], F32, name="kb_gpsimd")
            kb_share = kb_sb[t][:].rearrange("f b m -> f m b")[:, NX - M_GPSIMD : NX]
            if t == 0:
                nc.vector.tensor_copy(kb_gpsimd[:], kb_share)
            elif t == 1:
                nc.scalar.activation(kb_gpsimd[:], kb_share, COPY)
            else:
                nc.scalar.activation(kb_gpsimd[:, 1:M_GPSIMD], kb_share[:, 1:M_GPSIMD], COPY)
                nc.vector.tensor_copy(kb_gpsimd[:, 0:1], kb_share[:, 0:1])
            return kb_gpsimd

        def build_pair(t, kb_bank, kb_gpsimd):
            pair_flipped = pairs_flipped.tile([K, HALVES, G, NX, FG], F32, name="pair_flipped")
            kb_by_m = kb_sb[t][:].rearrange("f b m -> f m b")
            ka_by_m = ka_sb[t][:].rearrange("f a m -> f m a")
            pair_gpsimd = work.tile([F, M_GPSIMD, NX, NX], F32, name="pair_gpsimd")
            nc.gpsimd.tensor_tensor(
                pair_gpsimd[:],
                kb_gpsimd[:].unsqueeze(2).to_broadcast([F, M_GPSIMD, NX, NX]),
                ka_by_m[:, NX - M_GPSIMD : NX].unsqueeze(3).to_broadcast([F, M_GPSIMD, NX, NX]),
                MULT,
            )
            rows_of = []
            for half in range(HALVES):
                a_range = slice(half * A_HALF, (half + 1) * A_HALF)
                pair_vector = work.tile([F, M_VECTOR, A_HALF, NX], F32, name="pair_vector")
                from_sbuf = FLIPS if t == 0 and half == 0 else 0
                if from_sbuf:
                    vector_share(pair_vector, kb_by_m, ka_by_m[:, :, a_range], 0, from_sbuf)
                vector_share(pair_vector, kb_bank, ka_by_m[:, :, a_range], from_sbuf, M_VECTOR)
                rows_of.append(
                    [pair_vector[:, m] for m in range(M_VECTOR)] + [pair_gpsimd[:, m, a_range] for m in range(M_GPSIMD)]
                )
            all_vector = range(0, M_VECTOR // FLIPS * FLIPS, FLIPS)
            with_gpsimd = range(M_VECTOR // FLIPS * FLIPS, NX, FLIPS)
            for ms in (all_vector, with_gpsimd):
                for half in range(HALVES):
                    for m in ms:
                        flip_and_group(
                            nc,
                            flips,
                            identity,
                            [rows_of[half][m + i].rearrange("f a b -> f (a b)") for i in range(FLIPS)],
                            pair_flipped[:, half, :, m : m + FLIPS, :],
                        )
            return pair_flipped

        def look_up(t, r0, n_r, e_flipped):
            e_post = work.tile([F, n_r, HALVES, K], F32, name="e_post")
            nc.vector.tensor_tensor(
                e_post[:].rearrange("f r h k -> f (r h k)"),
                x_part[t // TERMS_OF_PART][:].indirect(offsets[:, r0 * AB // 16 : (r0 + n_r) * AB // 16]),
                scales_wide[t][:, 0:n_r].rearrange("f r k -> f (r k)"),
                MULT,
            )
            for half in range(HALVES):
                flip_and_group(
                    nc,
                    flips,
                    identity,
                    [e_post[:, i, half, :] for i in range(n_r)],
                    e_flipped[:, half, :, r0 : r0 + n_r, :],
                )

        def multiply(t, slots, e_flipped, pair_flipped):
            for half in range(HALVES):
                for s in slots:
                    for j in range(COL_TILES):
                        g = s * COL_TILES + j
                        nc.tensor.matmul(
                            products[s // BANK_SLOTS][j * TILE : (j + 1) * TILE, s % BANK_SLOTS, :],
                            e_flipped[:, half, g].rearrange("k r e -> k (r e)"),
                            pair_flipped[:, half, g].rearrange("k m e -> k e m"),
                            start=(t == 0 and half == 0 and s % BANK_SLOTS == 0),
                            stop=(t == T - 1 and half == HALVES - 1 and s % BANK_SLOTS == BANK_SLOTS - 1),
                        )

        kb_banks = [stage_kb(0), stage_kb(1)]
        kb_gpsimds = [stage_kb_gpsimd(0), stage_kb_gpsimd(1)]
        make_scales(0)
        pair_flipped_of = [build_pair(0, kb_banks[0], kb_gpsimds[0])]
        load_part(1)
        for t in range(2, T):
            load_kernels(t, nc.sync)
        for t in range(1, T):
            make_scales(t)
        e_flipped_before = None
        for t in range(T):
            if t + 2 < T:
                kb_banks.append(stage_kb(t + 2))
            if t + 1 < T:
                pair_flipped_of.append(build_pair(t + 1, kb_banks[t + 1], kb_gpsimds[t + 1]))
            e_flipped = flipped.tile([K, HALVES, G, NX, FG], F32, name="e_flipped")
            for r0 in range(0, NX, R_PIECE):
                if r0 + R_PIECE == NX and t + 2 < T:
                    kb_gpsimds.append(stage_kb_gpsimd(t + 2))
                if t == T - 1 and r0 + R_PIECE == NX:
                    look_up(t, r0, R_PIECE // 2, e_flipped)
                    look_up(t, r0 + R_PIECE // 2, R_PIECE // 2, e_flipped)
                else:
                    look_up(t, r0, R_PIECE, e_flipped)
                if t > 0:
                    multiply(t - 1, range(r0 * SLOTS // NX, (r0 + R_PIECE) * SLOTS // NX), e_flipped_before, pair_flipped_of[t - 1])
            e_flipped_before = e_flipped
        out_rows = out.rearrange("(e s j) c -> e s (j c)", e=FG, j=COL_TILES).rearrange("e s (q m) -> e q s m", m=NX)
        for b in range(PRODUCT_BANKS):
            slots = slice(b * BANK_SLOTS, (b + 1) * BANK_SLOTS)
            multiply(T - 1, range(slots.start, slots.stop), e_flipped_before, pair_flipped_of[T - 1])
            result = held.tile([F, BANK_SLOTS, FG, NX], F32, name=f"result{b}")
            nc.scalar.activation(result[:].rearrange("p s e m -> p s (e m)"), products[b][:], COPY)
            result_rows = result[:].rearrange("(q e) s c m -> e q s c m", e=FG)
            for e in range(FG):
                queue = nc.sync if e % 2 == 0 else nc.scalar
                queue.dma_start(out_rows[e, :, slots, :], result_rows[e, :, :, e, :])
